import numpy as np
import ml_dtypes


def mxq(x, axis, fmt="e4m3"):
    dtype, down = {"e4m3": (ml_dtypes.float8_e4m3fn, 7), "e5m2": (ml_dtypes.float8_e5m2, 14)}[fmt]
    v = np.moveaxis(np.asarray(x, np.float32).astype(ml_dtypes.bfloat16).astype(np.float64), axis, -1)
    blocks = v.reshape(v.shape[:-1] + (-1, 32))
    amax = np.abs(blocks).max(-1, keepdims=True)
    byte = np.maximum(np.where(amax > 0, np.frexp(amax)[1] - 1 + 127, 0) - down, 1)
    scale = np.exp2(byte - 127.0)
    codes = (blocks / scale).astype(np.float32).astype(dtype).astype(np.float64)
    return np.moveaxis((codes * scale).reshape(v.shape), -1, axis)


WIDE = False


def mx_kscale(k):
    if not WIDE:
        return np.ones(k)
    levels = np.array([10, -10, 5, -5, 0])
    if k % 512:
        return np.exp2(np.random.permutation(np.resize(levels, k // 32))).repeat(32)
    a = np.empty((k // 512, 16))
    for p in range(k // 512):
        a[p, :8] = np.random.permutation(np.resize(levels, 8))
        for g in range(8):
            far = levels[np.abs(levels - a[p, g]) >= 10]
            a[p, g + 8] = far[np.random.randint(len(far))]
    return np.exp2(a.ravel()).repeat(32)


BF16 = ml_dtypes.bfloat16


def bf(x):
    return np.asarray(x, np.float32).astype(BF16)


def f64(x):
    return np.asarray(x).astype(np.float64)


B, D_IN, HID, OUT = 512, 1024, 4096, 1024


def setup_inputs():
    s, t = mx_kscale(D_IN), mx_kscale(HID)
    u = np.concatenate([s, t])
    return {"x": bf(np.random.standard_normal((B, D_IN)) * s),
            "W1": bf(np.random.standard_normal((HID, D_IN)) / np.sqrt(D_IN) / s[None, :] * t[:, None]),
            "b1": bf(np.random.standard_normal(HID) * 0.3 * t),
            "W2": bf(np.random.standard_normal((OUT, D_IN + HID)) / np.sqrt(D_IN + HID) / u[None, :]),
            "b2": bf(np.random.standard_normal(OUT) * 0.3)}


def reference(x, W1, b1, W2, b2):
    xq = mxq(f64(x), 1, "e4m3")
    h1 = np.maximum((xq @ mxq(f64(W1), 1, "e4m3").T) + f64(b1), 0.0)
    concat = np.concatenate([xq, mxq(h1, 1, "e4m3")], axis=1)
    return (concat @ mxq(f64(W2), 1, "e4m3").T) + f64(b2)

@@ -1,0 +1,298 @@
+from contextlib import ExitStack
+
+import concourse.mybir as mybir
+from concourse.masks import make_identity
+
+F32 = mybir.dt.float32
+BF16 = mybir.dt.bfloat16
+U32 = mybir.dt.uint32
+U8 = mybir.dt.uint8
+FP8X4 = mybir.dt.float8_e4m3fn_x4
+ACT = mybir.ActivationFunctionType
+ALU = mybir.AluOpType
+
+P = 128
+B, D_IN, HID, OUT = 512, 1024, 4096, 1024
+FLOPS = 2 * B * (D_IN * HID + (D_IN + HID) * OUT)
+
+MANUAL = True
+RAW_BUFS = 9
+N_UNITS = 19
+
+
+def tile_dpn_kernel(tc, x, W1, b1, W2, b2, out):
+    nc = tc.nc
+    with ExitStack() as ctx:
+        const = ctx.enter_context(tc.tile_pool(name="const", bufs=1))
+        keep = ctx.enter_context(tc.tile_pool(name="keep", bufs=1))
+        rawp = ctx.enter_context(tc.tile_pool(name="rawp", bufs=RAW_BUFS))
+        grpp = ctx.enter_context(tc.tile_pool(name="grpp", bufs=3))
+        w1p = ctx.enter_context(tc.tile_pool(name="w1p", bufs=3))
+        hpp = ctx.enter_context(tc.tile_pool(name="hpp", bufs=3))
+        ostp = ctx.enter_context(tc.tile_pool(name="ostp", bufs=4))
+        psum = ctx.enter_context(tc.psum_pool(name="psum", bufs=4))
+        if MANUAL:
+            ctx.enter_context(tc.manual_schedule())
+
+        xc = keep.tile([P, 1024], U32, name="xc", align_bytes=64)
+        xs = keep.tile([P, 1024], U8, name="xs", align_bytes=64)
+        hc = keep.tile([P, 4096], U32, name="hc", align_bytes=64)
+        hs = keep.tile([P, 4096], U8, name="hs", align_bytes=64)
+        w2c = keep.tile([P, 10240], U32, name="w2c", align_bytes=64)
+        w2s = keep.tile([P, 10240], U8, name="w2s", align_bytes=64)
+
+        raws = {}
+        banks = {}
+        grps = {}
+        codes = {0: (xc[:], xs[:])}
+        for q in range(10):
+            codes[9 + q] = (
+                w2c[:, q * 1024 : (q + 1) * 1024],
+                w2s[:, q * 1024 : (q + 1) * 1024],
+            )
+
+        def load(k):
+            raw = rawp.tile([P, 4096], BF16, name="raw", tag="raw", align_bytes=64)
+            raws[k] = raw
+            if k == 0:
+                src = x.rearrange("(s p) k -> p s k", p=P)
+                dst = raw[:].rearrange("p (s k) -> p s k", s=4)
+                nc.sync.dma_start(out=dst[:, 0:2, :], in_=src[:, 0:2, :])
+                nc.sync.dma_start(out=dst[:, 2:4, :], in_=src[:, 2:4, :])
+            elif k < 9:
+                j = k - 1
+                src = W1[512 * j : 512 * (j + 1), :].rearrange("(p s) k -> p s k", s=4)
+                dst = raw[:].rearrange("p (s k) -> p s k", s=4)
+                if k == 1:
+                    nc.sync.dma_start(out=dst[:, 0:2, :], in_=src[:, 0:2, :])
+                    nc.sync.dma_start(out=dst[:, 2:4, :], in_=src[:, 2:4, :])
+                else:
+                    nc.sync.dma_start(out=dst, in_=src)
+            else:
+                n, c = divmod(k - 9, 5)
+                src = W2[
+                    512 * n : 512 * (n + 1), 1024 * c : 1024 * (c + 1)
+                ].rearrange("(s p) k -> p s k", p=P)
+                dst = raw[:].rearrange("p (s k) -> p s k", s=4)
+                nc.sync.dma_start(out=dst, in_=src)
+
+        def keep_warm(count):
+            for r in range(count):
+                nc.tensor.matmul(
+                    out=warm_ps[:], lhsT=ones[:], rhs=warm[:], start=True, stop=True
+                )
+
+        def transposes(k, mid=0):
+            rw = raws[k][:].bitcast(F32)
+            bl = []
+            for s in range(4):
+                if s == 2:
+                    keep_warm(mid)
+                bank = psum.tile([P, 512], F32, name="tb", tag="tb")
+                for q in range(4):
+                    nc.tensor.transpose(
+                        bank[:, q * P : (q + 1) * P],
+                        rw[
+                            :,
+                            s * 512 + (q // 2) * 256 + q % 2 : s * 512 + (q // 2 + 1) * 256 : 2,
+                        ],
+                        ident[:],
+                    )
+                bl.append(bank)
+            banks[k] = bl
+            grps[k] = grpp.tile([P, 4096], BF16, name="grp", tag="grp", align_bytes=64)
+
+        def evac(k, s, eng):
+            dst = grps[k][:].bitcast(F32).rearrange(
+                "p (g s r u) -> p g s r u", g=2, s=4, u=2
+            )[:, :, s]
+            src = banks[k][s][:].rearrange("p (g u r) -> p g r u", g=2, u=2)
+            if eng == "V":
+                nc.vector.tensor_copy(out=dst, in_=src)
+            else:
+                nc.scalar.copy(out=dst, in_=src)
+
+        def quant(k):
+            if 1 <= k < 9:
+                w1c = w1p.tile([P, 1024], U32, name="w1c", tag="w1c", align_bytes=64)
+                w1s = w1p.tile([P, 1024], U8, name="w1s", tag="w1s", align_bytes=64)
+                codes[k] = (w1c[:], w1s[:])
+            cd, sc = codes[k]
+            nc.vector.quantize_mx(out=cd.bitcast(FP8X4), scales=sc, in_=grps[k][:])
+
+        accs = {}
+        hps = {}
+        hgs = {}
+
+        def mm1(j):
+            cd, sc = codes[1 + j]
+            al = []
+            for t in range(4):
+                acc = psum.tile([P, 512], F32, name="mb", tag="mb")
+                for g in range(2):
+                    cols = slice(g * 512 + t * P, g * 512 + (t + 1) * P)
+                    nc.tensor.matmul_mx(
+                        out=acc[:],
+                        lhsT=cd[:, cols].bitcast(FP8X4),
+                        lhsT_scale=sc[:, cols],
+                        rhs=xc[:, g * 512 : (g + 1) * 512].bitcast(FP8X4),
+                        rhs_scale=xs[:, g * 512 : (g + 1) * 512],
+                        start=(g == 0),
+                        stop=(g == 1),
+                    )
+                al.append(acc)
+            accs[j] = al
+            hps[j] = hpp.tile([P, 2048], BF16, name="hp", tag="hp")
+
+        def relu(j, t, eng):
+            dst = hps[j][:, t * 512 : (t + 1) * 512]
+            bias = b1col[:, 4 * j + t : 4 * j + t + 1]
+            if eng == "V":
+                nc.vector.tensor_scalar(
+                    out=dst, in0=accs[j][t][:], scalar1=bias, scalar2=0.0,
+                    op0=ALU.add, op1=ALU.max,
+                )
+            else:
+                nc.scalar.activation(
+                    out=dst, in_=accs[j][t][:], func=ACT.Relu, bias=bias, scale=1.0
+                )
+
+        def regroup(j):
+            hg = hpp.tile([P, 2048], BF16, name="hg", tag="hg", align_bytes=64)
+            hgs[j] = hg
+            nc.vector.tensor_copy(
+                out=hg[:].rearrange("p (c i t) -> p c t i", i=4, t=4),
+                in_=hps[j][:].rearrange("p (t c i) -> p c t i", t=4, i=4),
+            )
+
+        def quant_h(j):
+            nc.vector.quantize_mx(
+                out=hc[:, j * 512 : (j + 1) * 512].bitcast(FP8X4),
+                scales=hs[:, j * 512 : (j + 1) * 512],
+                in_=hgs[j][:],
+            )
+
+        acc2 = {}
+
+        def mm2(n, c):
+            if c == 0:
+                acc2[n] = [
+                    psum.tile([P, 512], F32, name="mb", tag="mb") for bt in range(4)
+                ]
+            for bt in range(4):
+                for gg in (2 * c, 2 * c + 1):
+                    if gg < 2:
+                        lc, ls, base = xc, xs, gg * 512
+                    else:
+                        lc, ls, base = hc, hs, (gg - 2) * 512
+                    cols = slice(base + bt * P, base + (bt + 1) * P)
+                    rcols = slice(n * 5120 + gg * 512, n * 5120 + (gg + 1) * 512)
+                    nc.tensor.matmul_mx(
+                        out=acc2[n][bt][:],
+                        lhsT=lc[:, cols].bitcast(FP8X4),
+                        lhsT_scale=ls[:, cols],
+                        rhs=w2c[:, rcols].bitcast(FP8X4),
+                        rhs_scale=w2s[:, rcols],
+                        start=(gg == 0),
+                        stop=(gg == 9),
+                    )
+
+        def finish(n, bt):
+            ost = ostp.tile([P, 512], F32, name="ost", tag="ost")
+            nc.vector.tensor_tensor(
+                out=ost[:], in0=acc2[n][bt][:], in1=b2bc[:, n * 512 : (n + 1) * 512],
+                op=ALU.add,
+            )
+            nc.sync.dma_start(
+                out=out[bt * P : (bt + 1) * P, n * 512 : (n + 1) * 512], in_=ost[:]
+            )
+
+        b1z = const.tile([P, 512], BF16, name="b1z")
+        b2z = const.tile([P, OUT], BF16, name="b2z")
+        ones = const.tile([P, P], BF16, name="ones")
+        ident = const.tile([P, P], F32, name="ident")
+        b1col = const.tile([P, 32], F32, name="b1col")
+        b2bc = const.tile([P, OUT], F32, name="b2bc")
+        warm = const.tile([P, 512], BF16, name="warm")
+        tiny_in = const.tile([P, 8], F32, name="tiny_in")
+        tiny_out = const.tile([P, 8], F32, name="tiny_out")
+        nc.vector.memset(ones[:], 1.0)
+        nc.vector.memset(warm[:], 0.0)
+        nc.vector.memset(b1z[:], 0.0)
+        nc.vector.memset(b2z[:], 0.0)
+        nc.vector.memset(tiny_in[:], 0.0)
+        nc.scalar.dma_start(out=b1z[0:8, :], in_=b1.rearrange("(a w) -> a w", a=8))
+        nc.scalar.dma_start(out=b2z[0:1, :], in_=b2.rearrange("(o n) -> o n", o=1))
+        nc.scalar.activation(out=tiny_out[:], in_=tiny_in[:], func=ACT.Relu)
+        make_identity(nc, ident[:])
+
+        for k in range(RAW_BUFS):
+            load(k)
+
+        def next_load(k):
+            if k + RAW_BUFS < N_UNITS:
+                load(k + RAW_BUFS)
+
+        warm_ps = psum.tile([P, 512], F32, name="mb", tag="mb")
+        keep_warm(5)
+        transposes(0, 1)
+        next_load(0)
+        evac(0, 0, "V")
+        evac(0, 1, "S")
+        evac(0, 2, "V")
+        evac(0, 3, "S")
+        b1ps = psum.tile([P, 512], F32, name="mb", tag="mb")
+        for u in range(2):
+            nc.tensor.transpose(
+                b1ps[:, u * P : (u + 1) * P], b1z[:].bitcast(F32)[:, u:256:2], ident[:]
+            )
+        nc.vector.tensor_copy(
+            out=b1col[:].rearrange("p (j u e) -> p j u e", u=2, e=2),
+            in_=b1ps[:, 0 : 2 * P]
+            .bitcast(BF16)
+            .rearrange("p (u j e) -> p j u e", u=2, e=2)[:, 0:8],
+        )
+        for n in range(2):
+            b2ps = psum.tile([P, 512], F32, name="mb", tag="mb")
+            nc.tensor.matmul(
+                out=b2ps[:], lhsT=ones[:], rhs=b2z[:, n * 512 : (n + 1) * 512],
+                start=True, stop=True,
+            )
+            nc.scalar.copy(out=b2bc[:, n * 512 : (n + 1) * 512], in_=b2ps[:])
+        quant(0)
+        transposes(1, 1)
+        keep_warm(3)
+        next_load(1)
+        evac(1, 0, "V")
+        evac(1, 1, "S")
+        evac(1, 2, "V")
+        evac(1, 3, "S")
+        quant(1)
+
+        for p in range(18):
+            k = p + 2 if p + 2 < N_UNITS else None
+            if k is not None:
+                transposes(k)
+            if p + 2 < N_UNITS:
+                next_load(p + 2)
+            if p < 8:
+                mm1(p)
+            else:
+                mm2(*divmod(p - 8, 5))
+            if k is not None:
+                evac(k, 0, "V")
+                evac(k, 1, "S")
+                evac(k, 2, "S")
+                evac(k, 3, "S")
+            if 1 <= p <= 8:
+                regroup(p - 1)
+            if 2 <= p <= 9:
+                quant_h(p - 2)
+            if k is not None:
+                quant(k)
+            if p < 8:
+                for t in range(4):
+                    relu(p, t, "V" if (t == 3 and p % 2 == 1) else "S")
+            if p == 12 or p == 17:
+                for bt in range(4):
+                    finish((p - 8) // 5, bt)

@@ -17,6 +17,7 @@ FLOPS = 2 * B * (D_IN * HID + (D_IN + HID) * OUT)
 
 MANUAL = True
 RAW_BUFS = 9
+PERM_FROM = 9
 N_UNITS = 19
 
 
@@ -27,7 +28,8 @@ def tile_dpn_kernel(tc, x, W1, b1, W2, b2, out):
         keep = ctx.enter_context(tc.tile_pool(name="keep", bufs=1))
         rawp = ctx.enter_context(tc.tile_pool(name="rawp", bufs=RAW_BUFS))
         grpp = ctx.enter_context(tc.tile_pool(name="grpp", bufs=3))
-        w1p = ctx.enter_context(tc.tile_pool(name="w1p", bufs=3))
+        prmp = ctx.enter_context(tc.tile_pool(name="prmp", bufs=2))
+        wcp = ctx.enter_context(tc.tile_pool(name="wcp", bufs=3))
         hpp = ctx.enter_context(tc.tile_pool(name="hpp", bufs=3))
         ostp = ctx.enter_context(tc.tile_pool(name="ostp", bufs=4))
         psum = ctx.enter_context(tc.psum_pool(name="psum", bufs=4))
@@ -38,18 +40,11 @@ def tile_dpn_kernel(tc, x, W1, b1, W2, b2, out):
         xs = keep.tile([P, 1024], U8, name="xs", align_bytes=64)
         hc = keep.tile([P, 4096], U32, name="hc", align_bytes=64)
         hs = keep.tile([P, 4096], U8, name="hs", align_bytes=64)
-        w2c = keep.tile([P, 10240], U32, name="w2c", align_bytes=64)
-        w2s = keep.tile([P, 10240], U8, name="w2s", align_bytes=64)
 
         raws = {}
         banks = {}
         grps = {}
         codes = {0: (xc[:], xs[:])}
-        for q in range(10):
-            codes[9 + q] = (
-                w2c[:, q * 1024 : (q + 1) * 1024],
-                w2s[:, q * 1024 : (q + 1) * 1024],
-            )
 
         def load(k):
             raw = rawp.tile([P, 4096], BF16, name="raw", tag="raw", align_bytes=64)
@@ -82,22 +77,32 @@ def tile_dpn_kernel(tc, x, W1, b1, W2, b2, out):
                     out=warm_ps[:], lhsT=ones[:], rhs=warm[:], start=True, stop=True
                 )
 
+        prms = {}
+
+        def permute(k):
+            prm = prmp.tile([P, 4096], BF16, name="prm", tag="prm", align_bytes=64)
+            prms[k] = prm
+            nc.vector.tensor_copy(
+                out=prm[:].bitcast(F32).rearrange("p (g u w) -> p g u w", g=8, u=2),
+                in_=raws[k][:].bitcast(F32).rearrange("p (g w u) -> p g u w", g=8, u=2),
+            )
+
         def transposes(k, mid=0):
-            rw = raws[k][:].bitcast(F32)
+            rw = (prms[k] if k in prms else raws[k])[:].bitcast(F32)
             bl = []
             for s in range(4):
                 if s == 2:
                     keep_warm(mid)
                 bank = psum.tile([P, 512], F32, name="tb", tag="tb")
                 for q in range(4):
-                    nc.tensor.transpose(
-                        bank[:, q * P : (q + 1) * P],
-                        rw[
+                    if k in prms:
+                        words = rw[:, s * 512 + q * P : s * 512 + (q + 1) * P]
+                    else:
+                        words = rw[
                             :,
                             s * 512 + (q // 2) * 256 + q % 2 : s * 512 + (q // 2 + 1) * 256 : 2,
-                        ],
-                        ident[:],
-                    )
+                        ]
+                    nc.tensor.transpose(bank[:, q * P : (q + 1) * P], words, ident[:])
                 bl.append(bank)
             banks[k] = bl
             grps[k] = grpp.tile([P, 4096], BF16, name="grp", tag="grp", align_bytes=64)
@@ -113,10 +118,10 @@ def tile_dpn_kernel(tc, x, W1, b1, W2, b2, out):
                 nc.scalar.copy(out=dst, in_=src)
 
         def quant(k):
-            if 1 <= k < 9:
-                w1c = w1p.tile([P, 1024], U32, name="w1c", tag="w1c", align_bytes=64)
-                w1s = w1p.tile([P, 1024], U8, name="w1s", tag="w1s", align_bytes=64)
-                codes[k] = (w1c[:], w1s[:])
+            if k > 0:
+                wc = wcp.tile([P, 1024], U32, name="wc", tag="wc", align_bytes=64)
+                ws = wcp.tile([P, 1024], U8, name="ws", tag="ws", align_bytes=64)
+                codes[k] = (wc[:], ws[:])
             cd, sc = codes[k]
             nc.vector.quantize_mx(out=cd.bitcast(FP8X4), scales=sc, in_=grps[k][:])
 
@@ -175,6 +180,7 @@ def tile_dpn_kernel(tc, x, W1, b1, W2, b2, out):
         acc2 = {}
 
         def mm2(n, c):
+            w2c, w2s = codes[9 + 5 * n + c]
             if c == 0:
                 acc2[n] = [
                     psum.tile([P, 512], F32, name="mb", tag="mb") for bt in range(4)
@@ -186,7 +192,7 @@ def tile_dpn_kernel(tc, x, W1, b1, W2, b2, out):
                     else:
                         lc, ls, base = hc, hs, (gg - 2) * 512
                     cols = slice(base + bt * P, base + (bt + 1) * P)
-                    rcols = slice(n * 5120 + gg * 512, n * 5120 + (gg + 1) * 512)
+                    rcols = slice((gg % 2) * 512, (gg % 2 + 1) * 512)
                     nc.tensor.matmul_mx(
                         out=acc2[n][bt][:],
                         lhsT=lc[:, cols].bitcast(FP8X4),
@@ -281,6 +287,8 @@ def tile_dpn_kernel(tc, x, W1, b1, W2, b2, out):
                 mm2(*divmod(p - 8, 5))
             if k is not None:
                 evac(k, 0, "V")
+                if PERM_FROM <= k + 1 < N_UNITS:
+                    permute(k + 1)
                 evac(k, 1, "S")
                 evac(k, 2, "S")
                 evac(k, 3, "S")

@@ -52,8 +52,8 @@ def tile_dpn_kernel(tc, x, W1, b1, W2, b2, out):
             if k == 0:
                 src = x.rearrange("(s p) k -> p s k", p=P)
                 dst = raw[:].rearrange("p (s k) -> p s k", s=4)
-                nc.sync.dma_start(out=dst[:, 0:2, :], in_=src[:, 0:2, :])
-                nc.sync.dma_start(out=dst[:, 2:4, :], in_=src[:, 2:4, :])
+                for s in range(4):
+                    nc.sync.dma_start(out=dst[:, s, :], in_=src[:, s, :])
             elif k < 9:
                 j = k - 1
                 src = W1[512 * j : 512 * (j + 1), :].rearrange("(p s) k -> p s k", s=4)
@@ -74,18 +74,22 @@ def tile_dpn_kernel(tc, x, W1, b1, W2, b2, out):
         def keep_warm(count):
             for r in range(count):
                 nc.tensor.matmul(
-                    out=warm_ps[:], lhsT=ones[:], rhs=warm[:], start=True, stop=True
+                    out=warm_ps[:], lhsT=warm[:, 0:P], rhs=warm[:], start=True, stop=True
                 )
 
         prms = {}
 
-        def permute(k):
-            prm = prmp.tile([P, 4096], BF16, name="prm", tag="prm", align_bytes=64)
-            prms[k] = prm
-            nc.vector.tensor_copy(
-                out=prm[:].bitcast(F32).rearrange("p (g u w) -> p g u w", g=8, u=2),
-                in_=raws[k][:].bitcast(F32).rearrange("p (g w u) -> p g u w", g=8, u=2),
-            )
+        def permute(k, half, eng):
+            if half == 0:
+                prms[k] = prmp.tile([P, 4096], BF16, name="prm", tag="prm", align_bytes=64)
+            dst = prms[k][:, half * 2048 : (half + 1) * 2048].bitcast(F32)
+            src = raws[k][:, half * 2048 : (half + 1) * 2048].bitcast(F32)
+            dst = dst.rearrange("p (g u w) -> p g u w", g=4, u=2)
+            src = src.rearrange("p (g w u) -> p g u w", g=4, u=2)
+            if eng == "V":
+                nc.vector.tensor_copy(out=dst, in_=src)
+            else:
+                nc.scalar.copy(out=dst, in_=src)
 
         def transposes(k, mid=0):
             rw = (prms[k] if k in prms else raws[k])[:].bitcast(F32)
@@ -214,26 +218,24 @@ def tile_dpn_kernel(tc, x, W1, b1, W2, b2, out):
             )
 
         b1z = const.tile([P, 512], BF16, name="b1z")
-        b2z = const.tile([P, OUT], BF16, name="b2z")
-        ones = const.tile([P, P], BF16, name="ones")
         ident = const.tile([P, P], F32, name="ident")
         b1col = const.tile([P, 32], F32, name="b1col")
-        b2bc = const.tile([P, OUT], F32, name="b2bc")
+        b2bc = const.tile([P, OUT], BF16, name="b2bc")
         warm = const.tile([P, 512], BF16, name="warm")
         tiny_in = const.tile([P, 8], F32, name="tiny_in")
         tiny_out = const.tile([P, 8], F32, name="tiny_out")
-        nc.vector.memset(ones[:], 1.0)
+        nc.scalar.dma_start(
+            out=b1z[:],
+            in_=b1.rearrange("(o j w) -> o j w", o=1, j=8).broadcast_to([16, 8, 512]),
+        )
         nc.vector.memset(warm[:], 0.0)
-        nc.vector.memset(b1z[:], 0.0)
-        nc.vector.memset(b2z[:], 0.0)
         nc.vector.memset(tiny_in[:], 0.0)
-        nc.scalar.dma_start(out=b1z[0:8, :], in_=b1.rearrange("(a w) -> a w", a=8))
-        nc.scalar.dma_start(out=b2z[0:1, :], in_=b2.rearrange("(o n) -> o n", o=1))
         nc.scalar.activation(out=tiny_out[:], in_=tiny_in[:], func=ACT.Relu)
         make_identity(nc, ident[:])
 
         for k in range(RAW_BUFS):
             load(k)
+        nc.sync.dma_start(out=b2bc[:], in_=b2.partition_broadcast(P))
 
         def next_load(k):
             if k + RAW_BUFS < N_UNITS:
@@ -247,6 +249,15 @@ def tile_dpn_kernel(tc, x, W1, b1, W2, b2, out):
         evac(0, 1, "S")
         evac(0, 2, "V")
         evac(0, 3, "S")
+        quant(0)
+        transposes(1, 1)
+        keep_warm(3)
+        next_load(1)
+        evac(1, 0, "V")
+        evac(1, 1, "S")
+        evac(1, 2, "V")
+        evac(1, 3, "S")
+        quant(1)
         b1ps = psum.tile([P, 512], F32, name="mb", tag="mb")
         for u in range(2):
             nc.tensor.transpose(
@@ -258,22 +269,6 @@ def tile_dpn_kernel(tc, x, W1, b1, W2, b2, out):
             .bitcast(BF16)
             .rearrange("p (u j e) -> p j u e", u=2, e=2)[:, 0:8],
         )
-        for n in range(2):
-            b2ps = psum.tile([P, 512], F32, name="mb", tag="mb")
-            nc.tensor.matmul(
-                out=b2ps[:], lhsT=ones[:], rhs=b2z[:, n * 512 : (n + 1) * 512],
-                start=True, stop=True,
-            )
-            nc.scalar.copy(out=b2bc[:, n * 512 : (n + 1) * 512], in_=b2ps[:])
-        quant(0)
-        transposes(1, 1)
-        keep_warm(3)
-        next_load(1)
-        evac(1, 0, "V")
-        evac(1, 1, "S")
-        evac(1, 2, "V")
-        evac(1, 3, "S")
-        quant(1)
 
         for p in range(18):
             k = p + 2 if p + 2 < N_UNITS else None
@@ -287,18 +282,22 @@ def tile_dpn_kernel(tc, x, W1, b1, W2, b2, out):
                 mm2(*divmod(p - 8, 5))
             if k is not None:
                 evac(k, 0, "V")
-                if PERM_FROM <= k + 1 < N_UNITS:
-                    permute(k + 1)
+                permuting = PERM_FROM <= k + 1 < N_UNITS
+                if permuting:
+                    permute(k + 1, 0, "V")
                 evac(k, 1, "S")
                 evac(k, 2, "S")
                 evac(k, 3, "S")
+                if permuting:
+                    permute(k + 1, 1, "S")
+            if p >= 8 and k is not None:
+                quant(k)
             if 1 <= p <= 8:
                 regroup(p - 1)
             if 2 <= p <= 9:
                 quant_h(p - 2)
-            if k is not None:
-                quant(k)
             if p < 8:
+                quant(k)
                 for t in range(4):
                     relu(p, t, "V" if (t == 3 and p % 2 == 1) else "S")
             if p == 12 or p == 17:

@@ -17,7 +17,15 @@ FLOPS = 2 * B * (D_IN * HID + (D_IN + HID) * OUT)
 
 MANUAL = True
 RAW_BUFS = 9
+DV_UNITS = (18,)
 PERM_FROM = 9
+DV_STEPS = {
+    10: [("permute", 18, 0)],
+    11: [("permute", 18, 1), ("transpose", 18, 0)],
+    13: [("join", 18, 0)],
+    14: [("transpose", 18, 1)],
+    15: [("join", 18, 1)],
+}
 N_UNITS = 19
 
 
@@ -27,10 +35,11 @@ def tile_dpn_kernel(tc, x, W1, b1, W2, b2, out):
         const = ctx.enter_context(tc.tile_pool(name="const", bufs=1))
         keep = ctx.enter_context(tc.tile_pool(name="keep", bufs=1))
         rawp = ctx.enter_context(tc.tile_pool(name="rawp", bufs=RAW_BUFS))
-        grpp = ctx.enter_context(tc.tile_pool(name="grpp", bufs=3))
+        grpp = ctx.enter_context(tc.tile_pool(name="grpp", bufs=4))
         prmp = ctx.enter_context(tc.tile_pool(name="prmp", bufs=2))
         wcp = ctx.enter_context(tc.tile_pool(name="wcp", bufs=3))
         hpp = ctx.enter_context(tc.tile_pool(name="hpp", bufs=3))
+        dvp = ctx.enter_context(tc.tile_pool(name="dvp", bufs=2))
         ostp = ctx.enter_context(tc.tile_pool(name="ostp", bufs=4))
         psum = ctx.enter_context(tc.psum_pool(name="psum", bufs=4))
         if MANUAL:
@@ -63,6 +72,19 @@ def tile_dpn_kernel(tc, x, W1, b1, W2, b2, out):
                     nc.sync.dma_start(out=dst[:, 2:4, :], in_=src[:, 2:4, :])
                 else:
                     nc.sync.dma_start(out=dst, in_=src)
+            elif k in DV_UNITS:
+                n, c = divmod(k - 9, 5)
+                for g in range(2):
+                    for a in range(4):
+                        col = 1024 * c + 512 * g + P * a
+                        nc.sync.dma_start(
+                            out=raw[
+                                32 * a : 32 * (a + 1), g * 2048 : (g + 1) * 2048
+                            ].rearrange("p (h w) -> p h w", w=P),
+                            in_=W2[512 * n : 512 * (n + 1), col : col + P].rearrange(
+                                "(h j) w -> j h w", j=32
+                            ),
+                        )
             else:
                 n, c = divmod(k - 9, 5)
                 src = W2[
@@ -78,10 +100,13 @@ def tile_dpn_kernel(tc, x, W1, b1, W2, b2, out):
                 )
 
         prms = {}
+        permuted = set()
 
         def permute(k, half, eng):
-            if half == 0:
+            if k not in prms:
                 prms[k] = prmp.tile([P, 4096], BF16, name="prm", tag="prm", align_bytes=64)
+            permuted.add((k, 2 * half))
+            permuted.add((k, 2 * half + 1))
             dst = prms[k][:, half * 2048 : (half + 1) * 2048].bitcast(F32)
             src = raws[k][:, half * 2048 : (half + 1) * 2048].bitcast(F32)
             dst = dst.rearrange("p (g u w) -> p g u w", g=4, u=2)
@@ -91,21 +116,47 @@ def tile_dpn_kernel(tc, x, W1, b1, W2, b2, out):
             else:
                 nc.scalar.copy(out=dst, in_=src)
 
+        dvh = {}
+        dvt = {}
+
+        def dv_permute(k, g):
+            dvh[k, g] = dvp.tile([P, 2048], BF16, name="dvh", tag="dvh", align_bytes=64)
+            nc.scalar.copy(
+                out=dvh[k, g][:].bitcast(F32).rearrange("p (h u i) -> p h u i", u=2, i=32),
+                in_=raws[k][:, g * 2048 : (g + 1) * 2048]
+                .bitcast(F32)
+                .rearrange("p (h i u) -> p h u i", u=2, i=32),
+            )
+
+        def dv_transpose(k, g):
+            dvt[k, g] = dvp.tile([P, 2048], BF16, name="dvt", tag="dvt", align_bytes=64)
+            nc.vector.transpose(
+                out=dvt[k, g][:].bitcast(F32), in_=dvh[k, g][:].bitcast(F32)
+            )
+
+        def dv_join(k, g):
+            if g == 0:
+                grps[k] = grpp.tile([P, 4096], BF16, name="grp", tag="grp", align_bytes=64)
+            nc.scalar.copy(
+                out=grps[k][:, g * 2048 : (g + 1) * 2048]
+                .bitcast(F32)
+                .rearrange("p (h j u) -> p h j u", u=2, j=32),
+                in_=dvt[k, g][:].bitcast(F32).rearrange("p (h u j) -> p h j u", u=2, j=32),
+            )
+
         def transposes(k, mid=0):
-            rw = (prms[k] if k in prms else raws[k])[:].bitcast(F32)
             bl = []
             for s in range(4):
                 if s == 2:
                     keep_warm(mid)
                 bank = psum.tile([P, 512], F32, name="tb", tag="tb")
                 for q in range(4):
-                    if k in prms:
-                        words = rw[:, s * 512 + q * P : s * 512 + (q + 1) * P]
+                    if (k, s) in permuted:
+                        first = s * 512 + q * P
+                        words = prms[k][:].bitcast(F32)[:, first : first + P]
                     else:
-                        words = rw[
-                            :,
-                            s * 512 + (q // 2) * 256 + q % 2 : s * 512 + (q // 2 + 1) * 256 : 2,
-                        ]
+                        first = s * 512 + (q // 2) * 256
+                        words = raws[k][:].bitcast(F32)[:, first + q % 2 : first + 256 : 2]
                     nc.tensor.transpose(bank[:, q * P : (q + 1) * P], words, ident[:])
                 bl.append(bank)
             banks[k] = bl
@@ -153,18 +204,12 @@ def tile_dpn_kernel(tc, x, W1, b1, W2, b2, out):
             accs[j] = al
             hps[j] = hpp.tile([P, 2048], BF16, name="hp", tag="hp")
 
-        def relu(j, t, eng):
+        def relu(j, t):
             dst = hps[j][:, t * 512 : (t + 1) * 512]
             bias = b1col[:, 4 * j + t : 4 * j + t + 1]
-            if eng == "V":
-                nc.vector.tensor_scalar(
-                    out=dst, in0=accs[j][t][:], scalar1=bias, scalar2=0.0,
-                    op0=ALU.add, op1=ALU.max,
-                )
-            else:
-                nc.scalar.activation(
-                    out=dst, in_=accs[j][t][:], func=ACT.Relu, bias=bias, scale=1.0
-                )
+            nc.scalar.activation(
+                out=dst, in_=accs[j][t][:], func=ACT.Relu, bias=bias, scale=1.0
+            )
 
         def regroup(j):
             hg = hpp.tile([P, 2048], BF16, name="hg", tag="hg", align_bytes=64)
@@ -224,10 +269,8 @@ def tile_dpn_kernel(tc, x, W1, b1, W2, b2, out):
         warm = const.tile([P, 512], BF16, name="warm")
         tiny_in = const.tile([P, 8], F32, name="tiny_in")
         tiny_out = const.tile([P, 8], F32, name="tiny_out")
-        nc.scalar.dma_start(
-            out=b1z[:],
-            in_=b1.rearrange("(o j w) -> o j w", o=1, j=8).broadcast_to([16, 8, 512]),
-        )
+        nc.gpsimd.memset(b1z[:].bitcast(F32), 0.0)
+        nc.scalar.dma_start(out=b1z[0:8, :], in_=b1.rearrange("(a w) -> a w", a=8))
         nc.vector.memset(warm[:], 0.0)
         nc.vector.memset(tiny_in[:], 0.0)
         nc.scalar.activation(out=tiny_out[:], in_=tiny_in[:], func=ACT.Relu)
@@ -272,34 +315,42 @@ def tile_dpn_kernel(tc, x, W1, b1, W2, b2, out):
 
         for p in range(18):
             k = p + 2 if p + 2 < N_UNITS else None
-            if k is not None:
+            on_tensor = k is not None and k not in DV_UNITS
+            if on_tensor:
                 transposes(k)
-            if p + 2 < N_UNITS:
-                next_load(p + 2)
+            if k is not None:
+                next_load(k)
             if p < 8:
                 mm1(p)
             else:
                 mm2(*divmod(p - 8, 5))
-            if k is not None:
+            if k is not None and k + 1 < N_UNITS and k + 1 not in DV_UNITS:
+                permute(k + 1, 0, "V")
+            if on_tensor:
                 evac(k, 0, "V")
-                permuting = PERM_FROM <= k + 1 < N_UNITS
-                if permuting:
-                    permute(k + 1, 0, "V")
                 evac(k, 1, "S")
                 evac(k, 2, "S")
                 evac(k, 3, "S")
-                if permuting:
-                    permute(k + 1, 1, "S")
-            if p >= 8 and k is not None:
+            if k is not None and PERM_FROM <= k + 1 < N_UNITS and k + 1 not in DV_UNITS:
+                permute(k + 1, 1, "V" if k + 1 == 11 else "S")
+            if 1 <= p < 8:
+                regroup(p - 1)
+            if k is not None:
                 quant(k)
-            if 1 <= p <= 8:
+            for step, kd, g in DV_STEPS.get(p, ()):
+                if step == "permute":
+                    dv_permute(kd, g)
+                elif step == "transpose":
+                    dv_transpose(kd, g)
+                else:
+                    dv_join(kd, g)
+            if p == 8:
                 regroup(p - 1)
             if 2 <= p <= 9:
                 quant_h(p - 2)
             if p < 8:
-                quant(k)
                 for t in range(4):
-                    relu(p, t, "V" if (t == 3 and p % 2 == 1) else "S")
+                    relu(p, t)
             if p == 12 or p == 17:
                 for bt in range(4):
                     finish((p - 8) // 5, bt)

@@ -20,11 +20,10 @@ RAW_BUFS = 9
 DV_UNITS = (18,)
 PERM_FROM = 9
 DV_STEPS = {
-    10: [("permute", 18, 0)],
-    11: [("permute", 18, 1), ("transpose", 18, 0)],
-    13: [("join", 18, 0)],
-    14: [("transpose", 18, 1)],
-    15: [("join", 18, 1)],
+    12: [("permute", 18, 0)],
+    13: [("permute", 18, 1)],
+    14: [("transpose", 18, 0)],
+    15: [("transpose", 18, 1), ("join", 18, 0), ("join", 18, 1)],
 }
 N_UNITS = 19
 
@@ -38,7 +37,8 @@ def tile_dpn_kernel(tc, x, W1, b1, W2, b2, out):
         grpp = ctx.enter_context(tc.tile_pool(name="grpp", bufs=4))
         prmp = ctx.enter_context(tc.tile_pool(name="prmp", bufs=2))
         wcp = ctx.enter_context(tc.tile_pool(name="wcp", bufs=3))
-        hpp = ctx.enter_context(tc.tile_pool(name="hpp", bufs=3))
+        hpp = ctx.enter_context(tc.tile_pool(name="hpp", bufs=6))
+        hgp = ctx.enter_context(tc.tile_pool(name="hgp", bufs=3))
         dvp = ctx.enter_context(tc.tile_pool(name="dvp", bufs=2))
         ostp = ctx.enter_context(tc.tile_pool(name="ostp", bufs=4))
         psum = ctx.enter_context(tc.psum_pool(name="psum", bufs=4))
@@ -102,15 +102,14 @@ def tile_dpn_kernel(tc, x, W1, b1, W2, b2, out):
         prms = {}
         permuted = set()
 
-        def permute(k, half, eng):
+        def permute(k, first, count, eng):
             if k not in prms:
                 prms[k] = prmp.tile([P, 4096], BF16, name="prm", tag="prm", align_bytes=64)
-            permuted.add((k, 2 * half))
-            permuted.add((k, 2 * half + 1))
-            dst = prms[k][:, half * 2048 : (half + 1) * 2048].bitcast(F32)
-            src = raws[k][:, half * 2048 : (half + 1) * 2048].bitcast(F32)
-            dst = dst.rearrange("p (g u w) -> p g u w", g=4, u=2)
-            src = src.rearrange("p (g w u) -> p g u w", g=4, u=2)
+            for s in range(first, first + count):
+                permuted.add((k, s))
+            cols = slice(first * 1024, (first + count) * 1024)
+            dst = prms[k][:, cols].bitcast(F32).rearrange("p (g u w) -> p g u w", u=2, w=P)
+            src = raws[k][:, cols].bitcast(F32).rearrange("p (g w u) -> p g u w", u=2, w=P)
             if eng == "V":
                 nc.vector.tensor_copy(out=dst, in_=src)
             else:
@@ -204,15 +203,21 @@ def tile_dpn_kernel(tc, x, W1, b1, W2, b2, out):
             accs[j] = al
             hps[j] = hpp.tile([P, 2048], BF16, name="hp", tag="hp")
 
-        def relu(j, t):
+        def relu(j, t, eng):
             dst = hps[j][:, t * 512 : (t + 1) * 512]
             bias = b1col[:, 4 * j + t : 4 * j + t + 1]
-            nc.scalar.activation(
-                out=dst, in_=accs[j][t][:], func=ACT.Relu, bias=bias, scale=1.0
-            )
+            if eng == "V":
+                nc.vector.tensor_scalar(
+                    out=dst, in0=accs[j][t][:], scalar1=bias, scalar2=0.0,
+                    op0=ALU.add, op1=ALU.max,
+                )
+            else:
+                nc.scalar.activation(
+                    out=dst, in_=accs[j][t][:], func=ACT.Relu, bias=bias, scale=1.0
+                )
 
         def regroup(j):
-            hg = hpp.tile([P, 2048], BF16, name="hg", tag="hg", align_bytes=64)
+            hg = hgp.tile([P, 2048], BF16, name="hg", tag="hg", align_bytes=64)
             hgs[j] = hg
             nc.vector.tensor_copy(
                 out=hg[:].rearrange("p (c i t) -> p c t i", i=4, t=4),
@@ -286,19 +291,23 @@ def tile_dpn_kernel(tc, x, W1, b1, W2, b2, out):
 
         warm_ps = psum.tile([P, 512], F32, name="mb", tag="mb")
         keep_warm(5)
+        for s in range(4):
+            permute(0, s, 1, "V")
         transposes(0, 1)
         next_load(0)
-        evac(0, 0, "V")
+        evac(0, 0, "S")
         evac(0, 1, "S")
         evac(0, 2, "V")
         evac(0, 3, "S")
+        permute(1, 0, 2, "V")
+        permute(1, 2, 2, "S")
         quant(0)
         transposes(1, 1)
         keep_warm(3)
         next_load(1)
         evac(1, 0, "V")
         evac(1, 1, "S")
-        evac(1, 2, "V")
+        evac(1, 2, "S")
         evac(1, 3, "S")
         quant(1)
         b1ps = psum.tile([P, 512], F32, name="mb", tag="mb")
@@ -325,18 +334,19 @@ def tile_dpn_kernel(tc, x, W1, b1, W2, b2, out):
             else:
                 mm2(*divmod(p - 8, 5))
             if k is not None and k + 1 < N_UNITS and k + 1 not in DV_UNITS:
-                permute(k + 1, 0, "V")
+                permute(k + 1, 0, 2, "V")
             if on_tensor:
-                evac(k, 0, "V")
+                evac(k, 0, "S" if 8 <= p < 12 else "V")
                 evac(k, 1, "S")
                 evac(k, 2, "S")
                 evac(k, 3, "S")
             if k is not None and PERM_FROM <= k + 1 < N_UNITS and k + 1 not in DV_UNITS:
-                permute(k + 1, 1, "V" if k + 1 == 11 else "S")
-            if 1 <= p < 8:
-                regroup(p - 1)
-            if k is not None:
-                quant(k)
+                permute(k + 1, 2, 2, "V" if k + 1 == 11 else "S")
+            for j in range(8):
+                if p == (2 * j + 2 if j < 4 else j + 5) and j < 7:
+                    quant_h(j)
+                if p == (2 * j + 1 if j < 4 else j + 4):
+                    regroup(j)
             for step, kd, g in DV_STEPS.get(p, ()):
                 if step == "permute":
                     dv_permute(kd, g)
@@ -344,13 +354,13 @@ def tile_dpn_kernel(tc, x, W1, b1, W2, b2, out):
                     dv_transpose(kd, g)
                 else:
                     dv_join(kd, g)
-            if p == 8:
-                regroup(p - 1)
-            if 2 <= p <= 9:
-                quant_h(p - 2)
+            if k is not None:
+                quant(k)
+            if p == 11:
+                quant_h(7)
             if p < 8:
                 for t in range(4):
-                    relu(p, t)
+                    relu(p, t, "V" if t == 3 else "S")
             if p == 12 or p == 17:
                 for bt in range(4):
                     finish((p - 8) // 5, bt)

@@ -40,15 +40,15 @@ def tile_dpn_kernel(tc, x, W1, b1, W2, b2, out):
         hpp = ctx.enter_context(tc.tile_pool(name="hpp", bufs=6))
         hgp = ctx.enter_context(tc.tile_pool(name="hgp", bufs=3))
         dvp = ctx.enter_context(tc.tile_pool(name="dvp", bufs=2))
-        ostp = ctx.enter_context(tc.tile_pool(name="ostp", bufs=4))
+        ostp = ctx.enter_context(tc.tile_pool(name="ostp", bufs=6))
         psum = ctx.enter_context(tc.psum_pool(name="psum", bufs=4))
         if MANUAL:
             ctx.enter_context(tc.manual_schedule())
 
-        xc = keep.tile([P, 1024], U32, name="xc", align_bytes=64)
-        xs = keep.tile([P, 1024], U8, name="xs", align_bytes=64)
-        hc = keep.tile([P, 4096], U32, name="hc", align_bytes=64)
-        hs = keep.tile([P, 4096], U8, name="hs", align_bytes=64)
+        xc = keep.tile([P, 1024], U32, name="xc", align_bytes=256)
+        xs = keep.tile([P, 1024], U8, name="xs", align_bytes=256)
+        hc = keep.tile([P, 4096], U32, name="hc", align_bytes=256)
+        hs = keep.tile([P, 4096], U8, name="hs", align_bytes=256)
 
         raws = {}
         banks = {}
@@ -173,8 +173,8 @@ def tile_dpn_kernel(tc, x, W1, b1, W2, b2, out):
 
         def quant(k):
             if k > 0:
-                wc = wcp.tile([P, 1024], U32, name="wc", tag="wc", align_bytes=64)
-                ws = wcp.tile([P, 1024], U8, name="ws", tag="ws", align_bytes=64)
+                wc = wcp.tile([P, 1024], U32, name="wc", tag="wc", align_bytes=256)
+                ws = wcp.tile([P, 1024], U8, name="ws", tag="ws", align_bytes=256)
                 codes[k] = (wc[:], ws[:])
             cd, sc = codes[k]
             nc.vector.quantize_mx(out=cd.bitcast(FP8X4), scales=sc, in_=grps[k][:])
@@ -257,15 +257,14 @@ def tile_dpn_kernel(tc, x, W1, b1, W2, b2, out):
                         stop=(gg == 9),
                     )
 
-        def finish(n, bt):
-            ost = ostp.tile([P, 512], F32, name="ost", tag="ost")
+        def finish(n, bt, first, width):
+            ost = ostp.tile([P, width], F32, name="ost", tag="ost")
+            cols = slice(n * 512 + first, n * 512 + first + width)
             nc.vector.tensor_tensor(
-                out=ost[:], in0=acc2[n][bt][:], in1=b2bc[:, n * 512 : (n + 1) * 512],
+                out=ost[:], in0=acc2[n][bt][:, first : first + width], in1=b2bc[:, cols],
                 op=ALU.add,
             )
-            nc.sync.dma_start(
-                out=out[bt * P : (bt + 1) * P, n * 512 : (n + 1) * 512], in_=ost[:]
-            )
+            nc.sync.dma_start(out=out[bt * P : (bt + 1) * P, cols], in_=ost[:])
 
         b1z = const.tile([P, 512], BF16, name="b1z")
         ident = const.tile([P, P], F32, name="ident")
@@ -290,7 +289,7 @@ def tile_dpn_kernel(tc, x, W1, b1, W2, b2, out):
                 load(k + RAW_BUFS)
 
         warm_ps = psum.tile([P, 512], F32, name="mb", tag="mb")
-        keep_warm(5)
+        keep_warm(3)
         for s in range(4):
             permute(0, s, 1, "V")
         transposes(0, 1)
@@ -299,15 +298,13 @@ def tile_dpn_kernel(tc, x, W1, b1, W2, b2, out):
         evac(0, 1, "S")
         evac(0, 2, "V")
         evac(0, 3, "S")
-        permute(1, 0, 2, "V")
-        permute(1, 2, 2, "S")
         quant(0)
         transposes(1, 1)
-        keep_warm(3)
+        keep_warm(1)
         next_load(1)
         evac(1, 0, "V")
         evac(1, 1, "S")
-        evac(1, 2, "S")
+        evac(1, 2, "V")
         evac(1, 3, "S")
         quant(1)
         b1ps = psum.tile([P, 512], F32, name="mb", tag="mb")
@@ -363,4 +360,8 @@ def tile_dpn_kernel(tc, x, W1, b1, W2, b2, out):
                     relu(p, t, "V" if t == 3 else "S")
             if p == 12 or p == 17:
                 for bt in range(4):
-                    finish((p - 8) // 5, bt)
+                    if p == 17 and bt == 3:
+                        finish(1, bt, 0, 256)
+                        finish(1, bt, 256, 256)
+                    else:
+                        finish((p - 8) // 5, bt, 0, 512)

from contextlib import ExitStack

import concourse.mybir as mybir
from concourse.masks import make_identity

F32 = mybir.dt.float32
BF16 = mybir.dt.bfloat16
U32 = mybir.dt.uint32
U8 = mybir.dt.uint8
FP8X4 = mybir.dt.float8_e4m3fn_x4
ACT = mybir.ActivationFunctionType
ALU = mybir.AluOpType

P = 128
B, D_IN, HID, OUT = 512, 1024, 4096, 1024
FLOPS = 2 * B * (D_IN * HID + (D_IN + HID) * OUT)

MANUAL = True
RAW_BUFS = 9
DV_UNITS = (18,)
PERM_FROM = 9
DV_STEPS = {
    12: [("permute", 18, 0)],
    13: [("permute", 18, 1)],
    14: [("transpose", 18, 0)],
    15: [("transpose", 18, 1), ("join", 18, 0), ("join", 18, 1)],
}
N_UNITS = 19


def tile_dpn_kernel(tc, x, W1, b1, W2, b2, out):
    nc = tc.nc
    with ExitStack() as ctx:
        const = ctx.enter_context(tc.tile_pool(name="const", bufs=1))
        keep = ctx.enter_context(tc.tile_pool(name="keep", bufs=1))
        rawp = ctx.enter_context(tc.tile_pool(name="rawp", bufs=RAW_BUFS))
        grpp = ctx.enter_context(tc.tile_pool(name="grpp", bufs=4))
        prmp = ctx.enter_context(tc.tile_pool(name="prmp", bufs=2))
        wcp = ctx.enter_context(tc.tile_pool(name="wcp", bufs=3))
        hpp = ctx.enter_context(tc.tile_pool(name="hpp", bufs=6))
        hgp = ctx.enter_context(tc.tile_pool(name="hgp", bufs=3))
        dvp = ctx.enter_context(tc.tile_pool(name="dvp", bufs=2))
        ostp = ctx.enter_context(tc.tile_pool(name="ostp", bufs=6))
        psum = ctx.enter_context(tc.psum_pool(name="psum", bufs=4))
        if MANUAL:
            ctx.enter_context(tc.manual_schedule())

        xc = keep.tile([P, 1024], U32, name="xc", align_bytes=256)
        xs = keep.tile([P, 1024], U8, name="xs", align_bytes=256)
        hc = keep.tile([P, 4096], U32, name="hc", align_bytes=256)
        hs = keep.tile([P, 4096], U8, name="hs", align_bytes=256)

        raws = {}
        banks = {}
        grps = {}
        codes = {0: (xc[:], xs[:])}

        def load(k):
            raw = rawp.tile([P, 4096], BF16, name="raw", tag="raw", align_bytes=64)
            raws[k] = raw
            if k == 0:
                src = x.rearrange("(s p) k -> p s k", p=P)
                dst = raw[:].rearrange("p (s k) -> p s k", s=4)
                for s in range(4):
                    nc.sync.dma_start(out=dst[:, s, :], in_=src[:, s, :])
            elif k < 9:
                j = k - 1
                src = W1[512 * j : 512 * (j + 1), :].rearrange("(p s) k -> p s k", s=4)
                dst = raw[:].rearrange("p (s k) -> p s k", s=4)
                if k == 1:
                    nc.sync.dma_start(out=dst[:, 0:2, :], in_=src[:, 0:2, :])
                    nc.sync.dma_start(out=dst[:, 2:4, :], in_=src[:, 2:4, :])
                else:
                    nc.sync.dma_start(out=dst, in_=src)
            elif k in DV_UNITS:
                n, c = divmod(k - 9, 5)
                for g in range(2):
                    for a in range(4):
                        col = 1024 * c + 512 * g + P * a
                        nc.sync.dma_start(
                            out=raw[
                                32 * a : 32 * (a + 1), g * 2048 : (g + 1) * 2048
                            ].rearrange("p (h w) -> p h w", w=P),
                            in_=W2[512 * n : 512 * (n + 1), col : col + P].rearrange(
                                "(h j) w -> j h w", j=32
                            ),
                        )
            else:
                n, c = divmod(k - 9, 5)
                src = W2[
                    512 * n : 512 * (n + 1), 1024 * c : 1024 * (c + 1)
                ].rearrange("(s p) k -> p s k", p=P)
                dst = raw[:].rearrange("p (s k) -> p s k", s=4)
                nc.sync.dma_start(out=dst, in_=src)

        def keep_warm(count):
            for r in range(count):
                nc.tensor.matmul(
                    out=warm_ps[:], lhsT=warm[:, 0:P], rhs=warm[:], start=True, stop=True
                )

        prms = {}
        permuted = set()

        def permute(k, first, count, eng):
            if k not in prms:
                prms[k] = prmp.tile([P, 4096], BF16, name="prm", tag="prm", align_bytes=64)
            for s in range(first, first + count):
                permuted.add((k, s))
            cols = slice(first * 1024, (first + count) * 1024)
            dst = prms[k][:, cols].bitcast(F32).rearrange("p (g u w) -> p g u w", u=2, w=P)
            src = raws[k][:, cols].bitcast(F32).rearrange("p (g w u) -> p g u w", u=2, w=P)
            if eng == "V":
                nc.vector.tensor_copy(out=dst, in_=src)
            else:
                nc.scalar.copy(out=dst, in_=src)

        dvh = {}
        dvt = {}

        def dv_permute(k, g):
            dvh[k, g] = dvp.tile([P, 2048], BF16, name="dvh", tag="dvh", align_bytes=64)
            nc.scalar.copy(
                out=dvh[k, g][:].bitcast(F32).rearrange("p (h u i) -> p h u i", u=2, i=32),
                in_=raws[k][:, g * 2048 : (g + 1) * 2048]
                .bitcast(F32)
                .rearrange("p (h i u) -> p h u i", u=2, i=32),
            )

        def dv_transpose(k, g):
            dvt[k, g] = dvp.tile([P, 2048], BF16, name="dvt", tag="dvt", align_bytes=64)
            nc.vector.transpose(
                out=dvt[k, g][:].bitcast(F32), in_=dvh[k, g][:].bitcast(F32)
            )

        def dv_join(k, g):
            if g == 0:
                grps[k] = grpp.tile([P, 4096], BF16, name="grp", tag="grp", align_bytes=64)
            nc.scalar.copy(
                out=grps[k][:, g * 2048 : (g + 1) * 2048]
                .bitcast(F32)
                .rearrange("p (h j u) -> p h j u", u=2, j=32),
                in_=dvt[k, g][:].bitcast(F32).rearrange("p (h u j) -> p h j u", u=2, j=32),
            )

        def transposes(k, mid=0):
            bl = []
            for s in range(4):
                if s == 2:
                    keep_warm(mid)
                bank = psum.tile([P, 512], F32, name="tb", tag="tb")
                for q in range(4):
                    if (k, s) in permuted:
                        first = s * 512 + q * P
                        words = prms[k][:].bitcast(F32)[:, first : first + P]
                    else:
                        first = s * 512 + (q // 2) * 256
                        words = raws[k][:].bitcast(F32)[:, first + q % 2 : first + 256 : 2]
                    nc.tensor.transpose(bank[:, q * P : (q + 1) * P], words, ident[:])
                bl.append(bank)
            banks[k] = bl
            grps[k] = grpp.tile([P, 4096], BF16, name="grp", tag="grp", align_bytes=64)

        def evac(k, s, eng):
            dst = grps[k][:].bitcast(F32).rearrange(
                "p (g s r u) -> p g s r u", g=2, s=4, u=2
            )[:, :, s]
            src = banks[k][s][:].rearrange("p (g u r) -> p g r u", g=2, u=2)
            if eng == "V":
                nc.vector.tensor_copy(out=dst, in_=src)
            else:
                nc.scalar.copy(out=dst, in_=src)

        def quant(k):
            if k > 0:
                wc = wcp.tile([P, 1024], U32, name="wc", tag="wc", align_bytes=256)
                ws = wcp.tile([P, 1024], U8, name="ws", tag="ws", align_bytes=256)
                codes[k] = (wc[:], ws[:])
            cd, sc = codes[k]
            nc.vector.quantize_mx(out=cd.bitcast(FP8X4), scales=sc, in_=grps[k][:])

        accs = {}
        hps = {}
        hgs = {}

        def mm1(j):
            cd, sc = codes[1 + j]
            al = []
            for t in range(4):
                acc = psum.tile([P, 512], F32, name="mb", tag="mb")
                for g in range(2):
                    cols = slice(g * 512 + t * P, g * 512 + (t + 1) * P)
                    nc.tensor.matmul_mx(
                        out=acc[:],
                        lhsT=cd[:, cols].bitcast(FP8X4),
                        lhsT_scale=sc[:, cols],
                        rhs=xc[:, g * 512 : (g + 1) * 512].bitcast(FP8X4),
                        rhs_scale=xs[:, g * 512 : (g + 1) * 512],
                        start=(g == 0),
                        stop=(g == 1),
                    )
                al.append(acc)
            accs[j] = al
            hps[j] = hpp.tile([P, 2048], BF16, name="hp", tag="hp")

        def relu(j, t, eng):
            dst = hps[j][:, t * 512 : (t + 1) * 512]
            bias = b1col[:, 4 * j + t : 4 * j + t + 1]
            if eng == "V":
                nc.vector.tensor_scalar(
                    out=dst, in0=accs[j][t][:], scalar1=bias, scalar2=0.0,
                    op0=ALU.add, op1=ALU.max,
                )
            else:
                nc.scalar.activation(
                    out=dst, in_=accs[j][t][:], func=ACT.Relu, bias=bias, scale=1.0
                )

        def regroup(j):
            hg = hgp.tile([P, 2048], BF16, name="hg", tag="hg", align_bytes=64)
            hgs[j] = hg
            nc.vector.tensor_copy(
                out=hg[:].rearrange("p (c i t) -> p c t i", i=4, t=4),
                in_=hps[j][:].rearrange("p (t c i) -> p c t i", t=4, i=4),
            )

        def quant_h(j):
            nc.vector.quantize_mx(
                out=hc[:, j * 512 : (j + 1) * 512].bitcast(FP8X4),
                scales=hs[:, j * 512 : (j + 1) * 512],
                in_=hgs[j][:],
            )

        acc2 = {}

        def mm2(n, c):
            w2c, w2s = codes[9 + 5 * n + c]
            if c == 0:
                acc2[n] = [
                    psum.tile([P, 512], F32, name="mb", tag="mb") for bt in range(4)
                ]
            for bt in range(4):
                for gg in (2 * c, 2 * c + 1):
                    if gg < 2:
                        lc, ls, base = xc, xs, gg * 512
                    else:
                        lc, ls, base = hc, hs, (gg - 2) * 512
                    cols = slice(base + bt * P, base + (bt + 1) * P)
                    rcols = slice((gg % 2) * 512, (gg % 2 + 1) * 512)
                    nc.tensor.matmul_mx(
                        out=acc2[n][bt][:],
                        lhsT=lc[:, cols].bitcast(FP8X4),
                        lhsT_scale=ls[:, cols],
                        rhs=w2c[:, rcols].bitcast(FP8X4),
                        rhs_scale=w2s[:, rcols],
                        start=(gg == 0),
                        stop=(gg == 9),
                    )

        def finish(n, bt, first, width):
            ost = ostp.tile([P, width], F32, name="ost", tag="ost")
            cols = slice(n * 512 + first, n * 512 + first + width)
            nc.vector.tensor_tensor(
                out=ost[:], in0=acc2[n][bt][:, first : first + width], in1=b2bc[:, cols],
                op=ALU.add,
            )
            nc.sync.dma_start(out=out[bt * P : (bt + 1) * P, cols], in_=ost[:])

        b1z = const.tile([P, 512], BF16, name="b1z")
        ident = const.tile([P, P], F32, name="ident")
        b1col = const.tile([P, 32], F32, name="b1col")
        b2bc = const.tile([P, OUT], BF16, name="b2bc")
        warm = const.tile([P, 512], BF16, name="warm")
        tiny_in = const.tile([P, 8], F32, name="tiny_in")
        tiny_out = const.tile([P, 8], F32, name="tiny_out")
        nc.gpsimd.memset(b1z[:].bitcast(F32), 0.0)
        nc.scalar.dma_start(out=b1z[0:8, :], in_=b1.rearrange("(a w) -> a w", a=8))
        nc.vector.memset(warm[:], 0.0)
        nc.vector.memset(tiny_in[:], 0.0)
        nc.scalar.activation(out=tiny_out[:], in_=tiny_in[:], func=ACT.Relu)
        make_identity(nc, ident[:])

        for k in range(RAW_BUFS):
            load(k)
        nc.sync.dma_start(out=b2bc[:], in_=b2.partition_broadcast(P))

        def next_load(k):
            if k + RAW_BUFS < N_UNITS:
                load(k + RAW_BUFS)

        warm_ps = psum.tile([P, 512], F32, name="mb", tag="mb")
        keep_warm(3)
        for s in range(4):
            permute(0, s, 1, "V")
        transposes(0, 1)
        next_load(0)
        evac(0, 0, "S")
        evac(0, 1, "S")
        evac(0, 2, "V")
        evac(0, 3, "S")
        quant(0)
        transposes(1, 1)
        keep_warm(1)
        next_load(1)
        evac(1, 0, "V")
        evac(1, 1, "S")
        evac(1, 2, "V")
        evac(1, 3, "S")
        quant(1)
        b1ps = psum.tile([P, 512], F32, name="mb", tag="mb")
        for u in range(2):
            nc.tensor.transpose(
                b1ps[:, u * P : (u + 1) * P], b1z[:].bitcast(F32)[:, u:256:2], ident[:]
            )
        nc.vector.tensor_copy(
            out=b1col[:].rearrange("p (j u e) -> p j u e", u=2, e=2),
            in_=b1ps[:, 0 : 2 * P]
            .bitcast(BF16)
            .rearrange("p (u j e) -> p j u e", u=2, e=2)[:, 0:8],
        )

        for p in range(18):
            k = p + 2 if p + 2 < N_UNITS else None
            on_tensor = k is not None and k not in DV_UNITS
            if on_tensor:
                transposes(k)
            if k is not None:
                next_load(k)
            if p < 8:
                mm1(p)
            else:
                mm2(*divmod(p - 8, 5))
            if k is not None and k + 1 < N_UNITS and k + 1 not in DV_UNITS:
                permute(k + 1, 0, 2, "V")
            if on_tensor:
                evac(k, 0, "S" if 8 <= p < 12 else "V")
                evac(k, 1, "S")
                evac(k, 2, "S")
                evac(k, 3, "S")
            if k is not None and PERM_FROM <= k + 1 < N_UNITS and k + 1 not in DV_UNITS:
                permute(k + 1, 2, 2, "V" if k + 1 == 11 else "S")
            for j in range(8):
                if p == (2 * j + 2 if j < 4 else j + 5) and j < 7:
                    quant_h(j)
                if p == (2 * j + 1 if j < 4 else j + 4):
                    regroup(j)
            for step, kd, g in DV_STEPS.get(p, ()):
                if step == "permute":
                    dv_permute(kd, g)
                elif step == "transpose":
                    dv_transpose(kd, g)
                else:
                    dv_join(kd, g)
            if k is not None:
                quant(k)
            if p == 11:
                quant_h(7)
            if p < 8:
                for t in range(4):
                    relu(p, t, "V" if t == 3 else "S")
            if p == 12 or p == 17:
                for bt in range(4):
                    if p == 17 and bt == 3:
                        finish(1, bt, 0, 256)
                        finish(1, bt, 256, 256)
                    else:
                        finish((p - 8) // 5, bt, 0, 512)
